import numpy as np
import ml_dtypes


def mxq(x, axis, fmt="e4m3"):
    dtype, down = {"e4m3": (ml_dtypes.float8_e4m3fn, 7), "e5m2": (ml_dtypes.float8_e5m2, 14)}[fmt]
    v = np.moveaxis(np.asarray(x, np.float32).astype(ml_dtypes.bfloat16).astype(np.float64), axis, -1)
    blocks = v.reshape(v.shape[:-1] + (-1, 32))
    amax = np.abs(blocks).max(-1, keepdims=True)
    byte = np.maximum(np.where(amax > 0, np.frexp(amax)[1] - 1 + 127, 0) - down, 1)
    scale = np.exp2(byte - 127.0)
    codes = (blocks / scale).astype(np.float32).astype(dtype).astype(np.float64)
    return np.moveaxis((codes * scale).reshape(v.shape), -1, axis)


WIDE = False


def mx_kscale(k):
    if not WIDE:
        return np.ones(k)
    levels = np.array([10, -10, 5, -5, 0])
    a = np.random.permutation(np.resize(levels, k // 512 * 4)).reshape(k // 512, 4)
    idx = np.arange(k)
    return np.exp2(a[idx // 512, idx % 128 // 32])


BF16 = ml_dtypes.bfloat16


def bf(x):
    return np.asarray(x, np.float32).astype(BF16)


def f64(x):
    return np.asarray(x).astype(np.float64)


E2M1 = np.array([0.0, 0.5, 1.0, 1.5, 2.0, 3.0, 4.0, 6.0, -0.0, -0.5, -1.0, -1.5, -2.0, -3.0, -4.0, -6.0])


def pack_weight(w, fmt):
    k, n = w.shape
    w = f64(bf(w)).reshape(k // 32, 32, n)
    amax = np.abs(w).max(1)
    if fmt == "e4m3":
        byte = np.frexp(amax)[1] - 1 + 127 - 7
    else:
        mant, ex = np.frexp(amax / 6.0)
        byte = np.where(mant > 0.5, ex, ex - 1) + 127
    byte = np.clip(np.where(amax > 0, byte, 1), 1, 254)
    scaled = (w * np.exp2(127.0 - byte)[:, None, :]).reshape(k, n).astype(np.float32)
    by_word = np.ascontiguousarray(scaled.reshape(k // 512, 128, 4, n).transpose(0, 1, 3, 2))
    if fmt == "e4m3":
        words = by_word.astype(ml_dtypes.float8_e4m3fn).view(np.uint8)
    else:
        c = by_word.astype(ml_dtypes.float4_e2m1fn).view(np.uint8) & 0xF
        words = c[..., 0::2] | (c[..., 1::2] << 4)
    return np.ascontiguousarray(words), np.ascontiguousarray(byte.astype(np.uint8).reshape(k // 512, 16, n))


def unpack_weight(words, scales, fmt):
    g, p, n, _ = words.shape
    if fmt == "e4m3":
        vals = np.ascontiguousarray(words).view(ml_dtypes.float8_e4m3fn).astype(np.float64)
    else:
        nib = np.empty((g, p, n, 4), np.uint8)
        nib[..., 0::2] = words & 0xF
        nib[..., 1::2] = words >> 4
        vals = E2M1[nib]
    vals = vals * np.repeat(np.exp2(scales.astype(np.float64) - 127.0), 8, axis=1)[..., None]
    return vals.transpose(0, 1, 3, 2).reshape(g * 512, n)

def pack4(w):
    words, scales = pack_weight(w, "e2m1")
    return words.reshape(words.shape[0], 128, -1), scales


def unpack4(words, scales):
    return unpack_weight(words.reshape(words.shape[0], 128, -1, 2), scales, "e2m1")


T, HS, WS, WT, WH, WW, NH, HD, VID_DIM, TXT_DIM, TXT_LEN = 4, 4, 8, 4, 4, 4, 8, 128, 8192, 1536, 256
EPS = 1e-6
L_VID = T * HS * WS
N_WIN = (T // WT) * (HS // WH) * (WS // WW)
WIN_LEN = WT * WH * WW
INNER = NH * HD


def rmsnorm(x, gain):
    return x * (1.0 / np.sqrt(np.mean(x * x, axis=-1, keepdims=True) + EPS)) * gain


def window_partition(x):
    x = x.reshape(T // WT, WT, HS // WH, WH, WS // WW, WW, NH, HD)
    x = x.transpose(0, 2, 4, 1, 3, 5, 6, 7)
    return x.reshape(N_WIN, WIN_LEN, NH, HD)


def setup_inputs():
    s = mx_kscale(VID_DIM)
    vid = bf(np.random.standard_normal((L_VID, VID_DIM)) * s)
    words, scales = pack4(np.random.standard_normal((VID_DIM, 3 * INNER)) / np.sqrt(VID_DIM) / s[:, None])
    return {
        "vid": vid,
        "Wqkv_vid_words": words,
        "Wqkv_vid_scales": scales,
        "bqkv_vid": bf(0.1 * np.random.standard_normal(3 * INNER)),
        "q_scale_vid": bf(1.0 + 0.1 * np.random.standard_normal(HD)),
        "k_scale_vid": bf(1.0 + 0.1 * np.random.standard_normal(HD)),
    }


def reference(vid, Wqkv_vid_words, Wqkv_vid_scales, bqkv_vid, q_scale_vid, k_scale_vid):
    qkv = ((mxq(f64(vid), 1, "e4m3") @ unpack4(Wqkv_vid_words, Wqkv_vid_scales)) + f64(bqkv_vid)).reshape(L_VID, 3, NH, HD)
    q = rmsnorm(qkv[:, 0], f64(q_scale_vid))
    k = rmsnorm(qkv[:, 1], f64(k_scale_vid))
    return window_partition(q), window_partition(k), window_partition(qkv[:, 2])

@@ -1,0 +1,186 @@
+from contextlib import ExitStack
+
+import concourse.mybir as mybir
+from concourse.masks import make_identity
+
+F32 = mybir.dt.float32
+BF16 = mybir.dt.bfloat16
+I32 = mybir.dt.int32
+U32 = mybir.dt.uint32
+U8 = mybir.dt.uint8
+FP8X4 = mybir.dt.float8_e4m3fn_x4
+FP4X4 = mybir.dt.float4_e2m1fn_x4
+ALU = mybir.AluOpType
+ACT = mybir.ActivationFunctionType
+
+P = 128
+TOKENS = 128
+K = 8192
+K_PASS = 4 * P
+PASSES = K // K_PASS
+HEADS = 8
+HD = 128
+PART = HEADS * HD
+N_ALL = 3 * PART
+BANK = 512
+N_CONST = N_ALL + 2 * HD
+EPS = 1e-6
+HALF = PASSES // 2
+RUN_STEP = 4
+
+FLOPS = 2 * TOKENS * K * N_ALL
+
+
+def tile_naswinattention_pa_k_kernel(
+    tc, vid, w_words_in, w_scales_in, bias_in, q_gain_in, k_gain_in, out_q, out_k, out_v
+):
+    nc = tc.nc
+    with ExitStack() as ctx:
+        keep = ctx.enter_context(tc.tile_pool(name="keep", bufs=1))
+        stage = ctx.enter_context(tc.tile_pool(name="stage", bufs=4))
+        psum = ctx.enter_context(tc.psum_pool(name="psum", bufs=8))
+
+        x_rows = keep.tile([P, K], BF16)
+        x_codes = keep.tile([P, PASSES, TOKENS], U32, align_bytes=64)
+        x_planes = keep.tile([P, PASSES, TOKENS], U8, align_bytes=64)
+        w_words = keep.tile([P, PASSES, 2 * N_ALL], U8, align_bytes=64)
+        w_planes = keep.tile([P, PASSES, N_ALL], U8, align_bytes=64)
+        const_row = keep.tile([P, N_CONST], BF16)
+        const_all = keep.tile([P, N_CONST], BF16)
+
+        w_words_i32 = w_words[:].bitcast(I32)
+        w_planes_i32 = w_planes[:].bitcast(I32)
+        words_i32 = w_words_in.bitcast(I32)
+        scales_i32 = w_scales_in.bitcast(I32).rearrange("g q n -> q g n")
+
+        nc.vector.memset(w_planes_i32[:, 0:HALF, :], 0)
+        nc.vector.memset(const_row[:].bitcast(I32), 0)
+        nc.vector.memset(w_planes_i32[:, HALF:PASSES, :], 0)
+
+        ones = keep.tile([P, P], BF16)
+        nc.gpsimd.memset(ones[:], 1.0)
+        ident = keep.tile([P, P], F32)
+        make_identity(nc, ident[:])
+        to_window = keep.tile([P, P], F32)
+        nc.gpsimd.tensor_copy(
+            out=to_window[:].rearrange("l (n a c) -> l n a c", n=2, a=16, c=4),
+            in_=ident[:].rearrange("l (a n c) -> l n a c", a=16, n=2, c=4),
+        )
+
+        def load_scale_rows(first_pass):
+            for g in range(first_pass, first_pass + HALF, RUN_STEP):
+                for low in range(2):
+                    for r in range(4):
+                        nc.sync.dma_start(
+                            out=w_planes_i32[32 * low + r : P : 64, g : g + RUN_STEP, :],
+                            in_=scales_i32[4 * low + r : 16 : 8, g : g + RUN_STEP, :],
+                        )
+
+        def load_words(g, first_col, n_cols):
+            cols = slice(first_col // 2, (first_col + n_cols) // 2)
+            nc.sync.dma_start(out=w_words_i32[:, g, cols], in_=words_i32[g, :, cols])
+
+        for lo in range(0, K, 4 * K_PASS):
+            nc.sync.dma_start(out=x_rows[:, lo : lo + 4 * K_PASS], in_=vid[:, lo : lo + 4 * K_PASS])
+        for first_pass in range(0, PASSES, HALF):
+            load_scale_rows(first_pass)
+            for g in range(first_pass, first_pass + HALF):
+                load_words(g, 0, 2 * PART)
+        for g in range(PASSES):
+            load_words(g, 2 * PART, PART)
+
+        nc.scalar.dma_start(out=const_row[0:1, 0:N_ALL], in_=bias_in.rearrange("(o n) -> o n", o=1))
+        nc.scalar.dma_start(out=const_row[0:1, N_ALL : N_ALL + HD], in_=q_gain_in.rearrange("(o n) -> o n", o=1))
+        nc.scalar.dma_start(out=const_row[0:1, N_ALL + HD : N_CONST], in_=k_gain_in.rearrange("(o n) -> o n", o=1))
+
+        x_pairs = x_rows[:].bitcast(F32)
+        for j in range(PASSES // 2):
+            turned = psum.tile([P, 2, 2, TOKENS], F32, tag="bank")
+            for i in range(2):
+                g = 2 * j + i
+                for u in range(2):
+                    nc.tensor.transpose(
+                        out=turned[:, i, u, :],
+                        in_=x_pairs[:, 256 * g + u : 256 * (g + 1) : 2],
+                        identity=to_window[:],
+                    )
+            grouped = stage.tile([P, 2, TOKENS, 4], BF16, align_bytes=64)
+            copy_out = nc.vector.tensor_copy if j % 2 == 0 else nc.scalar.copy
+            copy_out(out=grouped[:].bitcast(F32), in_=turned[:].rearrange("p i u m -> p i m u"))
+            nc.vector.quantize_mx(
+                out=x_codes[:, 2 * j : 2 * j + 2, :].rearrange("p i m -> p (i m)").bitcast(FP8X4),
+                scales=x_planes[:, 2 * j : 2 * j + 2, :].rearrange("p i m -> p (i m)"),
+                in_=grouped[:].rearrange("p i m t -> p (i m t)"),
+            )
+
+        for lo in range(0, N_CONST, BANK):
+            width = min(BANK, N_CONST - lo)
+            spread = psum.tile([P, BANK], F32, tag="bank")
+            nc.tensor.matmul(
+                out=spread[:, 0:width], lhsT=ones[:], rhs=const_row[:, lo : lo + width], start=True, stop=True
+            )
+            nc.scalar.copy(out=const_all[:, lo : lo + width], in_=spread[:, 0:width])
+
+        def mx_passes(banks, first_col):
+            for g in range(PASSES):
+                for b, bank in enumerate(banks):
+                    col = first_col + b * BANK
+                    nc.tensor.matmul_mx(
+                        out=bank[:],
+                        lhsT=x_codes[:, g, :].bitcast(FP8X4),
+                        lhsT_scale=x_planes[:, g, :],
+                        rhs=w_words[:, g, 2 * col : 2 * (col + BANK)].bitcast(FP4X4),
+                        rhs_scale=w_planes[:, g, col : col + BANK],
+                        start=(g == 0),
+                        stop=(g == PASSES - 1),
+                    )
+
+        def add_bias(dst, bank, col):
+            nc.vector.tensor_tensor(out=dst, in0=bank[:], in1=const_all[:, col : col + BANK], op=ALU.add)
+
+        def finish_normed(banks, first_col, gain, out_rows, label):
+            y = keep.tile([P, PART], F32, name="y_" + label)
+            squares = keep.tile([P, PART], F32, name="squares_" + label)
+            sumsq = keep.tile([P, HEADS], F32, name="sumsq_" + label)
+            rms = keep.tile([P, HEADS], F32, name="rms_" + label)
+            rstd = keep.tile([P, HEADS], F32, name="rstd_" + label)
+            for b, bank in enumerate(banks):
+                add_bias(y[:, b * BANK : (b + 1) * BANK], bank, first_col + b * BANK)
+            for h in range(HEADS):
+                head = slice(h * HD, (h + 1) * HD)
+                nc.scalar.activation(
+                    out=squares[:, head], in_=y[:, head], func=ACT.Square, accum_out=sumsq[:, h : h + 1]
+                )
+            nc.vector.tensor_scalar(
+                out=rms[:], in0=sumsq[:], scalar1=1.0 / HD, scalar2=EPS, op0=ALU.mult, op1=ALU.add
+            )
+            nc.scalar.sqrt(out=rms[:], in_=rms[:])
+            nc.vector.reciprocal(out=rstd[:], in_=rms[:])
+            for h in range(HEADS):
+                head = slice(h * HD, (h + 1) * HD)
+                nc.vector.scalar_tensor_tensor(
+                    out=y[:, head],
+                    in0=y[:, head],
+                    scalar=rstd[:, h : h + 1],
+                    in1=gain,
+                    op0=ALU.mult,
+                    op1=ALU.mult,
+                )
+            nc.gpsimd.dma_start(out=out_rows, in_=y[:])
+
+        banks_qk = [psum.tile([P, BANK], F32, tag="bank", name="acc_qk%d" % b) for b in range(4)]
+        mx_passes(banks_qk, 0)
+        finish_normed(
+            banks_qk[0:2], 0, const_all[:, N_ALL : N_ALL + HD], out_q.rearrange("n p h d -> (n p) (h d)"), "q"
+        )
+        finish_normed(
+            banks_qk[2:4], PART, const_all[:, N_ALL + HD : N_CONST], out_k.rearrange("n p h d -> (n p) (h d)"), "k"
+        )
+
+        banks_v = [psum.tile([P, BANK], F32, tag="bank", name="acc_v%d" % b) for b in range(2)]
+        mx_passes(banks_v, 2 * PART)
+        out_v_rows = out_v.rearrange("n p h d -> (n p) (h d)")
+        for b, bank in enumerate(banks_v):
+            v = keep.tile([P, BANK], F32, name="v%d" % b)
+            add_bias(v[:], bank, 2 * PART + b * BANK)
+            nc.sync.dma_start(out=out_v_rows[:, b * BANK : (b + 1) * BANK], in_=v[:])

@@ -26,7 +26,6 @@ BANK = 512
 N_CONST = N_ALL + 2 * HD
 EPS = 1e-6
 HALF = PASSES // 2
-RUN_STEP = 4
 
 FLOPS = 2 * TOKENS * K * N_ALL
 
@@ -68,13 +67,11 @@ def tile_naswinattention_pa_k_kernel(
         )
 
         def load_scale_rows(first_pass):
-            for g in range(first_pass, first_pass + HALF, RUN_STEP):
-                for low in range(2):
-                    for r in range(4):
-                        nc.sync.dma_start(
-                            out=w_planes_i32[32 * low + r : P : 64, g : g + RUN_STEP, :],
-                            in_=scales_i32[4 * low + r : 16 : 8, g : g + RUN_STEP, :],
-                        )
+            passes = slice(first_pass, first_pass + HALF)
+            for r in range(8):
+                for q in (r, r + 8):
+                    row = 32 * (q // 4) + q % 4
+                    nc.sync.dma_start(out=w_planes_i32[row : row + 1, passes, :], in_=scales_i32[q : q + 1, passes, :])
 
         def load_words(g, first_col, n_cols):
             cols = slice(first_col // 2, (first_col + n_cols) // 2)

@@ -163,7 +163,7 @@ def tile_naswinattention_pa_k_kernel(
                     op0=ALU.mult,
                     op1=ALU.mult,
                 )
-            nc.gpsimd.dma_start(out=out_rows, in_=y[:])
+            nc.sync.dma_start(out=out_rows, in_=y[:])
 
         banks_qk = [psum.tile([P, BANK], F32, tag="bank", name="acc_qk%d" % b) for b in range(4)]
         mx_passes(banks_qk, 0)

@@ -25,7 +25,6 @@ N_ALL = 3 * PART
 BANK = 512
 N_CONST = N_ALL + 2 * HD
 EPS = 1e-6
-HALF = PASSES // 2
 
 FLOPS = 2 * TOKENS * K * N_ALL
 
@@ -52,9 +51,8 @@ def tile_naswinattention_pa_k_kernel(
         words_i32 = w_words_in.bitcast(I32)
         scales_i32 = w_scales_in.bitcast(I32).rearrange("g q n -> q g n")
 
-        nc.vector.memset(w_planes_i32[:, 0:HALF, :], 0)
+        nc.vector.memset(w_planes_i32[:], 0)
         nc.vector.memset(const_row[:].bitcast(I32), 0)
-        nc.vector.memset(w_planes_i32[:, HALF:PASSES, :], 0)
 
         ones = keep.tile([P, P], BF16)
         nc.gpsimd.memset(ones[:], 1.0)
@@ -66,12 +64,11 @@ def tile_naswinattention_pa_k_kernel(
             in_=ident[:].rearrange("l (a n c) -> l n a c", a=16, n=2, c=4),
         )
 
-        def load_scale_rows(first_pass):
-            passes = slice(first_pass, first_pass + HALF)
+        def load_scale_rows():
             for r in range(8):
                 for q in (r, r + 8):
                     row = 32 * (q // 4) + q % 4
-                    nc.sync.dma_start(out=w_planes_i32[row : row + 1, passes, :], in_=scales_i32[q : q + 1, passes, :])
+                    nc.sync.dma_start(out=w_planes_i32[row : row + 1, :, :], in_=scales_i32[q : q + 1, :, :])
 
         def load_words(g, first_col, n_cols):
             cols = slice(first_col // 2, (first_col + n_cols) // 2)
@@ -79,10 +76,9 @@ def tile_naswinattention_pa_k_kernel(
 
         for lo in range(0, K, 4 * K_PASS):
             nc.sync.dma_start(out=x_rows[:, lo : lo + 4 * K_PASS], in_=vid[:, lo : lo + 4 * K_PASS])
-        for first_pass in range(0, PASSES, HALF):
-            load_scale_rows(first_pass)
-            for g in range(first_pass, first_pass + HALF):
-                load_words(g, 0, 2 * PART)
+        load_scale_rows()
+        for g in range(PASSES):
+            load_words(g, 0, 2 * PART)
         for g in range(PASSES):
             load_words(g, 2 * PART, PART)
 

@@ -24,7 +24,9 @@ PART = HEADS * HD
 N_ALL = 3 * PART
 BANK = 512
 N_CONST = N_ALL + 2 * HD
+BIAS_ROWS = N_ALL // HD
 EPS = 1e-6
+HALF = PASSES // 2
 
 FLOPS = 2 * TOKENS * K * N_ALL
 
@@ -42,49 +44,65 @@ def tile_naswinattention_pa_k_kernel(
         x_codes = keep.tile([P, PASSES, TOKENS], U32, align_bytes=64)
         x_planes = keep.tile([P, PASSES, TOKENS], U8, align_bytes=64)
         w_words = keep.tile([P, PASSES, 2 * N_ALL], U8, align_bytes=64)
-        w_planes = keep.tile([P, PASSES, N_ALL], U8, align_bytes=64)
-        const_row = keep.tile([P, N_CONST], BF16)
+        planes_qk = keep.tile([P, PASSES, 2 * PART], U8, align_bytes=64)
+        planes_v = keep.tile([P, PASSES, PART], U8, align_bytes=64)
+        const_rows = keep.tile([P, HD], BF16)
         const_all = keep.tile([P, N_CONST], BF16)
 
         w_words_i32 = w_words[:].bitcast(I32)
-        w_planes_i32 = w_planes[:].bitcast(I32)
+        planes_qk_i32 = planes_qk[:].bitcast(I32)
+        planes_v_i32 = planes_v[:].bitcast(I32)
         words_i32 = w_words_in.bitcast(I32)
         scales_i32 = w_scales_in.bitcast(I32).rearrange("g q n -> q g n")
 
-        nc.vector.memset(w_planes_i32[:], 0)
-        nc.vector.memset(const_row[:].bitcast(I32), 0)
+        nc.vector.memset(const_rows[:].bitcast(I32), 0)
+        nc.vector.memset(planes_qk_i32[:, 0:HALF, :], 0)
 
-        ones = keep.tile([P, P], BF16)
-        nc.gpsimd.memset(ones[:], 1.0)
-        ident = keep.tile([P, P], F32)
-        make_identity(nc, ident[:])
-        to_window = keep.tile([P, P], F32)
-        nc.gpsimd.tensor_copy(
-            out=to_window[:].rearrange("l (n a c) -> l n a c", n=2, a=16, c=4),
-            in_=ident[:].rearrange("l (a n c) -> l n a c", a=16, n=2, c=4),
-        )
+        warm = keep.tile([P, 1], F32)
+        nc.vector.memset(warm[:], 1.0)
+        nc.scalar.sqrt(out=warm[:], in_=warm[:])
 
-        def load_scale_rows():
+        with tc.manual_schedule(engines={mybir.EngineType.Pool}):
+            ident = keep.tile([P, P], F32)
+            make_identity(nc, ident[:])
+            to_window = keep.tile([P, P], F32)
+            nc.gpsimd.tensor_copy(
+                out=to_window[:].rearrange("l (n a c) -> l n a c", n=2, a=16, c=4),
+                in_=ident[:].rearrange("l (a n c) -> l n a c", a=16, n=2, c=4),
+            )
+            nc.gpsimd.memset(planes_qk_i32[:, HALF:PASSES, :], 0)
+            nc.gpsimd.memset(planes_v_i32, 0)
+
+        def load_scale_rows(planes_i32, first_col, n_cols):
+            cols = slice(first_col // 4, (first_col + n_cols) // 4)
             for r in range(8):
                 for q in (r, r + 8):
                     row = 32 * (q // 4) + q % 4
-                    nc.sync.dma_start(out=w_planes_i32[row : row + 1, :, :], in_=scales_i32[q : q + 1, :, :])
+                    nc.sync.dma_start(out=planes_i32[row : row + 1, :, :], in_=scales_i32[q : q + 1, :, cols])
 
         def load_words(g, first_col, n_cols):
             cols = slice(first_col // 2, (first_col + n_cols) // 2)
             nc.sync.dma_start(out=w_words_i32[:, g, cols], in_=words_i32[g, :, cols])
 
-        for lo in range(0, K, 4 * K_PASS):
-            nc.sync.dma_start(out=x_rows[:, lo : lo + 4 * K_PASS], in_=vid[:, lo : lo + 4 * K_PASS])
-        load_scale_rows()
-        for g in range(PASSES):
-            load_words(g, 0, 2 * PART)
-        for g in range(PASSES):
-            load_words(g, 2 * PART, PART)
+        with tc.manual_schedule(engines={mybir.EngineType.SP}):
+            for lo in range(0, K, 4 * K_PASS):
+                nc.sync.dma_start(out=x_rows[:, lo : lo + 4 * K_PASS], in_=vid[:, lo : lo + 4 * K_PASS])
+            load_scale_rows(planes_qk_i32, 0, 2 * PART)
+            for g in range(PASSES):
+                load_words(g, 0, 2 * PART)
+            load_scale_rows(planes_v_i32, 2 * PART, PART)
+            for g in range(PASSES):
+                load_words(g, 2 * PART, PART)
 
-        nc.scalar.dma_start(out=const_row[0:1, 0:N_ALL], in_=bias_in.rearrange("(o n) -> o n", o=1))
-        nc.scalar.dma_start(out=const_row[0:1, N_ALL : N_ALL + HD], in_=q_gain_in.rearrange("(o n) -> o n", o=1))
-        nc.scalar.dma_start(out=const_row[0:1, N_ALL + HD : N_CONST], in_=k_gain_in.rearrange("(o n) -> o n", o=1))
+        nc.scalar.dma_start(out=const_rows[0:BIAS_ROWS, :], in_=bias_in.rearrange("(r n) -> r n", n=HD))
+        nc.scalar.dma_start(
+            out=const_rows[BIAS_ROWS : BIAS_ROWS + 1, :], in_=q_gain_in.rearrange("(r n) -> r n", r=1)
+        )
+        nc.scalar.dma_start(
+            out=const_rows[BIAS_ROWS + 1 : BIAS_ROWS + 2, :], in_=k_gain_in.rearrange("(r n) -> r n", r=1)
+        )
+        ident_bf = keep.tile([P, P], BF16)
+        nc.scalar.copy(out=ident_bf[:], in_=ident[:])
 
         x_pairs = x_rows[:].bitcast(F32)
         for j in range(PASSES // 2):
@@ -109,12 +127,18 @@ def tile_naswinattention_pa_k_kernel(
         for lo in range(0, N_CONST, BANK):
             width = min(BANK, N_CONST - lo)
             spread = psum.tile([P, BANK], F32, tag="bank")
-            nc.tensor.matmul(
-                out=spread[:, 0:width], lhsT=ones[:], rhs=const_row[:, lo : lo + width], start=True, stop=True
-            )
+            for at in range(0, width, HD):
+                r = (lo + at) // HD
+                nc.tensor.matmul(
+                    out=spread[:, at : at + HD],
+                    lhsT=ident_bf[:, r : r + 1].to_broadcast([P, P]),
+                    rhs=const_rows[:],
+                    start=True,
+                    stop=True,
+                )
             nc.scalar.copy(out=const_all[:, lo : lo + width], in_=spread[:, 0:width])
 
-        def mx_passes(banks, first_col):
+        def mx_passes(banks, planes, first_col):
             for g in range(PASSES):
                 for b, bank in enumerate(banks):
                     col = first_col + b * BANK
@@ -123,7 +147,7 @@ def tile_naswinattention_pa_k_kernel(
                         lhsT=x_codes[:, g, :].bitcast(FP8X4),
                         lhsT_scale=x_planes[:, g, :],
                         rhs=w_words[:, g, 2 * col : 2 * (col + BANK)].bitcast(FP4X4),
-                        rhs_scale=w_planes[:, g, col : col + BANK],
+                        rhs_scale=planes[:, g, b * BANK : (b + 1) * BANK],
                         start=(g == 0),
                         stop=(g == PASSES - 1),
                     )
@@ -162,7 +186,7 @@ def tile_naswinattention_pa_k_kernel(
             nc.sync.dma_start(out=out_rows, in_=y[:])
 
         banks_qk = [psum.tile([P, BANK], F32, tag="bank", name="acc_qk%d" % b) for b in range(4)]
-        mx_passes(banks_qk, 0)
+        mx_passes(banks_qk, planes_qk, 0)
         finish_normed(
             banks_qk[0:2], 0, const_all[:, N_ALL : N_ALL + HD], out_q.rearrange("n p h d -> (n p) (h d)"), "q"
         )
@@ -171,7 +195,7 @@ def tile_naswinattention_pa_k_kernel(
         )
 
         banks_v = [psum.tile([P, BANK], F32, tag="bank", name="acc_v%d" % b) for b in range(2)]
-        mx_passes(banks_v, 2 * PART)
+        mx_passes(banks_v, planes_v, 2 * PART)
         out_v_rows = out_v.rearrange("n p h d -> (n p) (h d)")
         for b, bank in enumerate(banks_v):
             v = keep.tile([P, BANK], F32, name="v%d" % b)

@@ -44,19 +44,17 @@ def tile_naswinattention_pa_k_kernel(
         x_codes = keep.tile([P, PASSES, TOKENS], U32, align_bytes=64)
         x_planes = keep.tile([P, PASSES, TOKENS], U8, align_bytes=64)
         w_words = keep.tile([P, PASSES, 2 * N_ALL], U8, align_bytes=64)
-        planes_qk = keep.tile([P, PASSES, 2 * PART], U8, align_bytes=64)
-        planes_v = keep.tile([P, PASSES, PART], U8, align_bytes=64)
+        w_planes = keep.tile([P, PASSES, N_ALL], U8, align_bytes=64)
         const_rows = keep.tile([P, HD], BF16)
         const_all = keep.tile([P, N_CONST], BF16)
 
         w_words_i32 = w_words[:].bitcast(I32)
-        planes_qk_i32 = planes_qk[:].bitcast(I32)
-        planes_v_i32 = planes_v[:].bitcast(I32)
+        w_planes_i32 = w_planes[:].bitcast(I32)
         words_i32 = w_words_in.bitcast(I32)
         scales_i32 = w_scales_in.bitcast(I32).rearrange("g q n -> q g n")
 
         nc.vector.memset(const_rows[:].bitcast(I32), 0)
-        nc.vector.memset(planes_qk_i32[:, 0:HALF, :], 0)
+        nc.vector.memset(w_planes_i32[:, 0:HALF, :], 0)
 
         warm = keep.tile([P, 1], F32)
         nc.vector.memset(warm[:], 1.0)
@@ -70,15 +68,13 @@ def tile_naswinattention_pa_k_kernel(
                 out=to_window[:].rearrange("l (n a c) -> l n a c", n=2, a=16, c=4),
                 in_=ident[:].rearrange("l (a n c) -> l n a c", a=16, n=2, c=4),
             )
-            nc.gpsimd.memset(planes_qk_i32[:, HALF:PASSES, :], 0)
-            nc.gpsimd.memset(planes_v_i32, 0)
+            for g in range(HALF, PASSES, 2):
+                nc.gpsimd.memset(w_planes_i32[:, g : g + 2, :], 0)
 
-        def load_scale_rows(planes_i32, first_col, n_cols):
-            cols = slice(first_col // 4, (first_col + n_cols) // 4)
-            for r in range(8):
-                for q in (r, r + 8):
-                    row = 32 * (q // 4) + q % 4
-                    nc.sync.dma_start(out=planes_i32[row : row + 1, :, :], in_=scales_i32[q : q + 1, :, cols])
+        def load_scale_row(q, first_pass):
+            passes = slice(first_pass, first_pass + HALF)
+            row = 32 * (q // 4) + q % 4
+            nc.sync.dma_start(out=w_planes_i32[row : row + 1, passes, :], in_=scales_i32[q : q + 1, passes, :])
 
         def load_words(g, first_col, n_cols):
             cols = slice(first_col // 2, (first_col + n_cols) // 2)
@@ -87,10 +83,15 @@ def tile_naswinattention_pa_k_kernel(
         with tc.manual_schedule(engines={mybir.EngineType.SP}):
             for lo in range(0, K, 4 * K_PASS):
                 nc.sync.dma_start(out=x_rows[:, lo : lo + 4 * K_PASS], in_=vid[:, lo : lo + 4 * K_PASS])
-            load_scale_rows(planes_qk_i32, 0, 2 * PART)
-            for g in range(PASSES):
+            for r in range(8):
+                load_scale_row(r, 0)
+                load_scale_row(r + 8, 0)
+            for g in range(HALF):
                 load_words(g, 0, 2 * PART)
-            load_scale_rows(planes_v_i32, 2 * PART, PART)
+                load_scale_row(g, HALF)
+                load_scale_row(g + 8, HALF)
+            for g in range(HALF, PASSES):
+                load_words(g, 0, 2 * PART)
             for g in range(PASSES):
                 load_words(g, 2 * PART, PART)
 
@@ -138,7 +139,7 @@ def tile_naswinattention_pa_k_kernel(
                 )
             nc.scalar.copy(out=const_all[:, lo : lo + width], in_=spread[:, 0:width])
 
-        def mx_passes(banks, planes, first_col):
+        def mx_passes(banks, first_col):
             for g in range(PASSES):
                 for b, bank in enumerate(banks):
                     col = first_col + b * BANK
@@ -147,7 +148,7 @@ def tile_naswinattention_pa_k_kernel(
                         lhsT=x_codes[:, g, :].bitcast(FP8X4),
                         lhsT_scale=x_planes[:, g, :],
                         rhs=w_words[:, g, 2 * col : 2 * (col + BANK)].bitcast(FP4X4),
-                        rhs_scale=planes[:, g, b * BANK : (b + 1) * BANK],
+                        rhs_scale=w_planes[:, g, col : col + BANK],
                         start=(g == 0),
                         stop=(g == PASSES - 1),
                     )
@@ -186,7 +187,7 @@ def tile_naswinattention_pa_k_kernel(
             nc.sync.dma_start(out=out_rows, in_=y[:])
 
         banks_qk = [psum.tile([P, BANK], F32, tag="bank", name="acc_qk%d" % b) for b in range(4)]
-        mx_passes(banks_qk, planes_qk, 0)
+        mx_passes(banks_qk, 0)
         finish_normed(
             banks_qk[0:2], 0, const_all[:, N_ALL : N_ALL + HD], out_q.rearrange("n p h d -> (n p) (h d)"), "q"
         )
@@ -195,7 +196,7 @@ def tile_naswinattention_pa_k_kernel(
         )
 
         banks_v = [psum.tile([P, BANK], F32, tag="bank", name="acc_v%d" % b) for b in range(2)]
-        mx_passes(banks_v, planes_v, 2 * PART)
+        mx_passes(banks_v, 2 * PART)
         out_v_rows = out_v.rearrange("n p h d -> (n p) (h d)")
         for b, bank in enumerate(banks_v):
             v = keep.tile([P, BANK], F32, name="v%d" % b)

@@ -27,6 +27,7 @@ N_CONST = N_ALL + 2 * HD
 BIAS_ROWS = N_ALL // HD
 EPS = 1e-6
 HALF = PASSES // 2
+WHOLE = 4
 
 FLOPS = 2 * TOKENS * K * N_ALL
 
@@ -43,12 +44,13 @@ def tile_naswinattention_pa_k_kernel(
         x_rows = keep.tile([P, K], BF16)
         x_codes = keep.tile([P, PASSES, TOKENS], U32, align_bytes=64)
         x_planes = keep.tile([P, PASSES, TOKENS], U8, align_bytes=64)
-        w_words = keep.tile([P, PASSES, 2 * N_ALL], U8, align_bytes=64)
+        words_whole = keep.tile([P, WHOLE, 2 * N_ALL], U8, align_bytes=64)
+        words_qk = keep.tile([P, PASSES - WHOLE, 2 * 2 * PART], U8, align_bytes=64)
+        words_v = keep.tile([P, PASSES - WHOLE, 2 * PART], U8, align_bytes=64)
         w_planes = keep.tile([P, PASSES, N_ALL], U8, align_bytes=64)
         const_rows = keep.tile([P, HD], BF16)
         const_all = keep.tile([P, N_CONST], BF16)
 
-        w_words_i32 = w_words[:].bitcast(I32)
         w_planes_i32 = w_planes[:].bitcast(I32)
         words_i32 = w_words_in.bitcast(I32)
         scales_i32 = w_scales_in.bitcast(I32).rearrange("g q n -> q g n")
@@ -76,9 +78,13 @@ def tile_naswinattention_pa_k_kernel(
             row = 32 * (q // 4) + q % 4
             nc.sync.dma_start(out=w_planes_i32[row : row + 1, passes, :], in_=scales_i32[q : q + 1, passes, :])
 
-        def load_words(g, first_col, n_cols):
+        def load_words(words, g, n_passes, first_col, n_cols):
+            at = g if g < WHOLE else g - WHOLE
             cols = slice(first_col // 2, (first_col + n_cols) // 2)
-            nc.sync.dma_start(out=w_words_i32[:, g, cols], in_=words_i32[g, :, cols])
+            nc.sync.dma_start(
+                out=words[:].bitcast(I32)[:, at : at + n_passes, :],
+                in_=words_i32[g : g + n_passes, :, cols].rearrange("g p n -> p g n"),
+            )
 
         with tc.manual_schedule(engines={mybir.EngineType.SP}):
             for lo in range(0, K, 4 * K_PASS):
@@ -86,14 +92,18 @@ def tile_naswinattention_pa_k_kernel(
             for r in range(8):
                 load_scale_row(r, 0)
                 load_scale_row(r + 8, 0)
-            for g in range(HALF):
-                load_words(g, 0, 2 * PART)
-                load_scale_row(g, HALF)
-                load_scale_row(g + 8, HALF)
-            for g in range(HALF, PASSES):
-                load_words(g, 0, 2 * PART)
             for g in range(PASSES):
-                load_words(g, 2 * PART, PART)
+                if g < WHOLE:
+                    load_words(words_whole, g, 1, 0, N_ALL)
+                else:
+                    load_words(words_qk, g, 1, 0, 2 * PART)
+                if g < HALF:
+                    load_scale_row(g, HALF)
+                    load_scale_row(g + 8, HALF)
+            for g in range(WHOLE, PASSES - 2, 2):
+                load_words(words_v, g, 2, 2 * PART, PART)
+            for g in range(PASSES - 2, PASSES):
+                load_words(words_v, g, 1, 2 * PART, PART)
 
         nc.scalar.dma_start(out=const_rows[0:BIAS_ROWS, :], in_=bias_in.rearrange("(r n) -> r n", n=HD))
         nc.scalar.dma_start(
@@ -139,16 +149,15 @@ def tile_naswinattention_pa_k_kernel(
                 )
             nc.scalar.copy(out=const_all[:, lo : lo + width], in_=spread[:, 0:width])
 
-        def mx_passes(banks, first_col):
-            for g in range(PASSES):
-                for b, bank in enumerate(banks):
-                    col = first_col + b * BANK
+        def mx_passes(passes, bank_numbers, words, first_pass):
+            for g in passes:
+                for i, b in enumerate(bank_numbers):
                     nc.tensor.matmul_mx(
-                        out=bank[:],
+                        out=banks[b][:],
                         lhsT=x_codes[:, g, :].bitcast(FP8X4),
                         lhsT_scale=x_planes[:, g, :],
-                        rhs=w_words[:, g, 2 * col : 2 * (col + BANK)].bitcast(FP4X4),
-                        rhs_scale=w_planes[:, g, col : col + BANK],
+                        rhs=words[:, g - first_pass, 2 * i * BANK : 2 * (i + 1) * BANK].bitcast(FP4X4),
+                        rhs_scale=w_planes[:, g, b * BANK : (b + 1) * BANK],
                         start=(g == 0),
                         stop=(g == PASSES - 1),
                     )
@@ -186,19 +195,19 @@ def tile_naswinattention_pa_k_kernel(
                 )
             nc.sync.dma_start(out=out_rows, in_=y[:])
 
-        banks_qk = [psum.tile([P, BANK], F32, tag="bank", name="acc_qk%d" % b) for b in range(4)]
-        mx_passes(banks_qk, 0)
+        banks = [psum.tile([P, BANK], F32, tag="bank", name="acc%d" % b) for b in range(6)]
+        mx_passes(range(WHOLE), range(6), words_whole, 0)
+        mx_passes(range(WHOLE, PASSES), range(4), words_qk, WHOLE)
         finish_normed(
-            banks_qk[0:2], 0, const_all[:, N_ALL : N_ALL + HD], out_q.rearrange("n p h d -> (n p) (h d)"), "q"
+            banks[0:2], 0, const_all[:, N_ALL : N_ALL + HD], out_q.rearrange("n p h d -> (n p) (h d)"), "q"
         )
         finish_normed(
-            banks_qk[2:4], PART, const_all[:, N_ALL + HD : N_CONST], out_k.rearrange("n p h d -> (n p) (h d)"), "k"
+            banks[2:4], PART, const_all[:, N_ALL + HD : N_CONST], out_k.rearrange("n p h d -> (n p) (h d)"), "k"
         )
 
-        banks_v = [psum.tile([P, BANK], F32, tag="bank", name="acc_v%d" % b) for b in range(2)]
-        mx_passes(banks_v, 2 * PART)
+        mx_passes(range(WHOLE, PASSES), range(4, 6), words_v, WHOLE)
         out_v_rows = out_v.rearrange("n p h d -> (n p) (h d)")
-        for b, bank in enumerate(banks_v):
+        for b, bank in enumerate(banks[4:6]):
             v = keep.tile([P, BANK], F32, name="v%d" % b)
             add_bias(v[:], bank, 2 * PART + b * BANK)
             nc.sync.dma_start(out=out_v_rows[:, b * BANK : (b + 1) * BANK], in_=v[:])

from contextlib import ExitStack

import concourse.mybir as mybir
from concourse.masks import make_identity

F32 = mybir.dt.float32
BF16 = mybir.dt.bfloat16
I32 = mybir.dt.int32
U32 = mybir.dt.uint32
U8 = mybir.dt.uint8
FP8X4 = mybir.dt.float8_e4m3fn_x4
FP4X4 = mybir.dt.float4_e2m1fn_x4
ALU = mybir.AluOpType
ACT = mybir.ActivationFunctionType

P = 128
TOKENS = 128
K = 8192
K_PASS = 4 * P
PASSES = K // K_PASS
HEADS = 8
HD = 128
PART = HEADS * HD
N_ALL = 3 * PART
BANK = 512
N_CONST = N_ALL + 2 * HD
BIAS_ROWS = N_ALL // HD
EPS = 1e-6
HALF = PASSES // 2
WHOLE = 4

FLOPS = 2 * TOKENS * K * N_ALL


def tile_naswinattention_pa_k_kernel(
    tc, vid, w_words_in, w_scales_in, bias_in, q_gain_in, k_gain_in, out_q, out_k, out_v
):
    nc = tc.nc
    with ExitStack() as ctx:
        keep = ctx.enter_context(tc.tile_pool(name="keep", bufs=1))
        stage = ctx.enter_context(tc.tile_pool(name="stage", bufs=4))
        psum = ctx.enter_context(tc.psum_pool(name="psum", bufs=8))

        x_rows = keep.tile([P, K], BF16)
        x_codes = keep.tile([P, PASSES, TOKENS], U32, align_bytes=64)
        x_planes = keep.tile([P, PASSES, TOKENS], U8, align_bytes=64)
        words_whole = keep.tile([P, WHOLE, 2 * N_ALL], U8, align_bytes=64)
        words_qk = keep.tile([P, PASSES - WHOLE, 2 * 2 * PART], U8, align_bytes=64)
        words_v = keep.tile([P, PASSES - WHOLE, 2 * PART], U8, align_bytes=64)
        w_planes = keep.tile([P, PASSES, N_ALL], U8, align_bytes=64)
        const_rows = keep.tile([P, HD], BF16)
        const_all = keep.tile([P, N_CONST], BF16)

        w_planes_i32 = w_planes[:].bitcast(I32)
        words_i32 = w_words_in.bitcast(I32)
        scales_i32 = w_scales_in.bitcast(I32).rearrange("g q n -> q g n")

        nc.vector.memset(const_rows[:].bitcast(I32), 0)
        nc.vector.memset(w_planes_i32[:, 0:HALF, :], 0)

        warm = keep.tile([P, 1], F32)
        nc.vector.memset(warm[:], 1.0)
        nc.scalar.sqrt(out=warm[:], in_=warm[:])

        with tc.manual_schedule(engines={mybir.EngineType.Pool}):
            ident = keep.tile([P, P], F32)
            make_identity(nc, ident[:])
            to_window = keep.tile([P, P], F32)
            nc.gpsimd.tensor_copy(
                out=to_window[:].rearrange("l (n a c) -> l n a c", n=2, a=16, c=4),
                in_=ident[:].rearrange("l (a n c) -> l n a c", a=16, n=2, c=4),
            )
            for g in range(HALF, PASSES, 2):
                nc.gpsimd.memset(w_planes_i32[:, g : g + 2, :], 0)

        def load_scale_row(q, first_pass):
            passes = slice(first_pass, first_pass + HALF)
            row = 32 * (q // 4) + q % 4
            nc.sync.dma_start(out=w_planes_i32[row : row + 1, passes, :], in_=scales_i32[q : q + 1, passes, :])

        def load_words(words, g, n_passes, first_col, n_cols):
            at = g if g < WHOLE else g - WHOLE
            cols = slice(first_col // 2, (first_col + n_cols) // 2)
            nc.sync.dma_start(
                out=words[:].bitcast(I32)[:, at : at + n_passes, :],
                in_=words_i32[g : g + n_passes, :, cols].rearrange("g p n -> p g n"),
            )

        with tc.manual_schedule(engines={mybir.EngineType.SP}):
            for lo in range(0, K, 4 * K_PASS):
                nc.sync.dma_start(out=x_rows[:, lo : lo + 4 * K_PASS], in_=vid[:, lo : lo + 4 * K_PASS])
            for r in range(8):
                load_scale_row(r, 0)
                load_scale_row(r + 8, 0)
            for g in range(PASSES):
                if g < WHOLE:
                    load_words(words_whole, g, 1, 0, N_ALL)
                else:
                    load_words(words_qk, g, 1, 0, 2 * PART)
                if g < HALF:
                    load_scale_row(g, HALF)
                    load_scale_row(g + 8, HALF)
            for g in range(WHOLE, PASSES - 2, 2):
                load_words(words_v, g, 2, 2 * PART, PART)
            for g in range(PASSES - 2, PASSES):
                load_words(words_v, g, 1, 2 * PART, PART)

        nc.scalar.dma_start(out=const_rows[0:BIAS_ROWS, :], in_=bias_in.rearrange("(r n) -> r n", n=HD))
        nc.scalar.dma_start(
            out=const_rows[BIAS_ROWS : BIAS_ROWS + 1, :], in_=q_gain_in.rearrange("(r n) -> r n", r=1)
        )
        nc.scalar.dma_start(
            out=const_rows[BIAS_ROWS + 1 : BIAS_ROWS + 2, :], in_=k_gain_in.rearrange("(r n) -> r n", r=1)
        )
        ident_bf = keep.tile([P, P], BF16)
        nc.scalar.copy(out=ident_bf[:], in_=ident[:])

        x_pairs = x_rows[:].bitcast(F32)
        for j in range(PASSES // 2):
            turned = psum.tile([P, 2, 2, TOKENS], F32, tag="bank")
            for i in range(2):
                g = 2 * j + i
                for u in range(2):
                    nc.tensor.transpose(
                        out=turned[:, i, u, :],
                        in_=x_pairs[:, 256 * g + u : 256 * (g + 1) : 2],
                        identity=to_window[:],
                    )
            grouped = stage.tile([P, 2, TOKENS, 4], BF16, align_bytes=64)
            copy_out = nc.vector.tensor_copy if j % 2 == 0 else nc.scalar.copy
            copy_out(out=grouped[:].bitcast(F32), in_=turned[:].rearrange("p i u m -> p i m u"))
            nc.vector.quantize_mx(
                out=x_codes[:, 2 * j : 2 * j + 2, :].rearrange("p i m -> p (i m)").bitcast(FP8X4),
                scales=x_planes[:, 2 * j : 2 * j + 2, :].rearrange("p i m -> p (i m)"),
                in_=grouped[:].rearrange("p i m t -> p (i m t)"),
            )

        for lo in range(0, N_CONST, BANK):
            width = min(BANK, N_CONST - lo)
            spread = psum.tile([P, BANK], F32, tag="bank")
            for at in range(0, width, HD):
                r = (lo + at) // HD
                nc.tensor.matmul(
                    out=spread[:, at : at + HD],
                    lhsT=ident_bf[:, r : r + 1].to_broadcast([P, P]),
                    rhs=const_rows[:],
                    start=True,
                    stop=True,
                )
            nc.scalar.copy(out=const_all[:, lo : lo + width], in_=spread[:, 0:width])

        def mx_passes(passes, bank_numbers, words, first_pass):
            for g in passes:
                for i, b in enumerate(bank_numbers):
                    nc.tensor.matmul_mx(
                        out=banks[b][:],
                        lhsT=x_codes[:, g, :].bitcast(FP8X4),
                        lhsT_scale=x_planes[:, g, :],
                        rhs=words[:, g - first_pass, 2 * i * BANK : 2 * (i + 1) * BANK].bitcast(FP4X4),
                        rhs_scale=w_planes[:, g, b * BANK : (b + 1) * BANK],
                        start=(g == 0),
                        stop=(g == PASSES - 1),
                    )

        def add_bias(dst, bank, col):
            nc.vector.tensor_tensor(out=dst, in0=bank[:], in1=const_all[:, col : col + BANK], op=ALU.add)

        def finish_normed(banks, first_col, gain, out_rows, label):
            y = keep.tile([P, PART], F32, name="y_" + label)
            squares = keep.tile([P, PART], F32, name="squares_" + label)
            sumsq = keep.tile([P, HEADS], F32, name="sumsq_" + label)
            rms = keep.tile([P, HEADS], F32, name="rms_" + label)
            rstd = keep.tile([P, HEADS], F32, name="rstd_" + label)
            for b, bank in enumerate(banks):
                add_bias(y[:, b * BANK : (b + 1) * BANK], bank, first_col + b * BANK)
            for h in range(HEADS):
                head = slice(h * HD, (h + 1) * HD)
                nc.scalar.activation(
                    out=squares[:, head], in_=y[:, head], func=ACT.Square, accum_out=sumsq[:, h : h + 1]
                )
            nc.vector.tensor_scalar(
                out=rms[:], in0=sumsq[:], scalar1=1.0 / HD, scalar2=EPS, op0=ALU.mult, op1=ALU.add
            )
            nc.scalar.sqrt(out=rms[:], in_=rms[:])
            nc.vector.reciprocal(out=rstd[:], in_=rms[:])
            for h in range(HEADS):
                head = slice(h * HD, (h + 1) * HD)
                nc.vector.scalar_tensor_tensor(
                    out=y[:, head],
                    in0=y[:, head],
                    scalar=rstd[:, h : h + 1],
                    in1=gain,
                    op0=ALU.mult,
                    op1=ALU.mult,
                )
            nc.sync.dma_start(out=out_rows, in_=y[:])

        banks = [psum.tile([P, BANK], F32, tag="bank", name="acc%d" % b) for b in range(6)]
        mx_passes(range(WHOLE), range(6), words_whole, 0)
        mx_passes(range(WHOLE, PASSES), range(4), words_qk, WHOLE)
        finish_normed(
            banks[0:2], 0, const_all[:, N_ALL : N_ALL + HD], out_q.rearrange("n p h d -> (n p) (h d)"), "q"
        )
        finish_normed(
            banks[2:4], PART, const_all[:, N_ALL + HD : N_CONST], out_k.rearrange("n p h d -> (n p) (h d)"), "k"
        )

        mx_passes(range(WHOLE, PASSES), range(4, 6), words_v, WHOLE)
        out_v_rows = out_v.rearrange("n p h d -> (n p) (h d)")
        for b, bank in enumerate(banks[4:6]):
            v = keep.tile([P, BANK], F32, name="v%d" % b)
            add_bias(v[:], bank, 2 * PART + b * BANK)
            nc.sync.dma_start(out=out_v_rows[:, b * BANK : (b + 1) * BANK], in_=v[:])
